import numpy as np
import ml_dtypes


def mxq(x, axis, fmt="e4m3"):
    dtype, down = {"e4m3": (ml_dtypes.float8_e4m3fn, 7), "e5m2": (ml_dtypes.float8_e5m2, 14)}[fmt]
    v = np.moveaxis(np.asarray(x, np.float32).astype(ml_dtypes.bfloat16).astype(np.float64), axis, -1)
    blocks = v.reshape(v.shape[:-1] + (-1, 32))
    amax = np.abs(blocks).max(-1, keepdims=True)
    byte = np.maximum(np.where(amax > 0, np.frexp(amax)[1] - 1 + 127, 0) - down, 1)
    scale = np.exp2(byte - 127.0)
    codes = (blocks / scale).astype(np.float32).astype(dtype).astype(np.float64)
    return np.moveaxis((codes * scale).reshape(v.shape), -1, axis)


WIDE = False


def mx_kscale(k):
    if not WIDE:
        return np.ones(k)
    levels = np.array([10, -10, 5, -5, 0])
    a = np.random.permutation(np.resize(levels, k // 512 * 4)).reshape(k // 512, 4)
    idx = np.arange(k)
    return np.exp2(a[idx // 512, idx % 128 // 32])


BF16 = ml_dtypes.bfloat16


def bf(x):
    return np.asarray(x, np.float32).astype(BF16)


def f64(x):
    return np.asarray(x).astype(np.float64)


B, T, E, C, H, XB = 1, 512, 2048, 2048, 16, 512
D = C // H


def decay_mask():
    gamma = 1.0 - 2.0 ** (-5.0 - f64(np.arange(H)))
    idx = np.arange(T)
    diff = idx[:, None] - idx[None, :]
    ex = f64(np.where(diff >= 0, diff, 0))
    return np.where(diff[None] >= 0, gamma[:, None, None] ** ex[None], 0.0)


def setup_inputs():
    s = mx_kscale(T)
    return {"q_rot": bf(np.random.standard_normal((B, T, C)) * 0.4),
            "k_rot": bf(np.random.standard_normal((B, T, C)) * 0.4 * s[None, :, None]),
            "v": bf(np.random.standard_normal((B, T, C)) * 0.5 / s[None, :, None])}


def reference(q_rot, k_rot, v):
    q = f64(q_rot).reshape(B, T, H, D).transpose(0, 2, 1, 3)
    k = f64(k_rot).reshape(B, T, H, D).transpose(0, 2, 1, 3)
    vh = f64(v).reshape(B, T, H, D).transpose(0, 2, 1, 3)
    scores = (q @ k.transpose(0, 1, 3, 2)) * (D ** -0.5)
    sm = scores * decay_mask()[None]
    y = mxq(sm, 3, "e4m3") @ mxq(vh, 2, "e4m3")
    return y.transpose(0, 2, 1, 3).reshape(B, T, C)

@@ -1,0 +1,178 @@
+import math
+from contextlib import ExitStack
+
+import concourse.mybir as mybir
+from concourse.masks import make_identity
+
+BF16 = mybir.dt.bfloat16
+F32 = mybir.dt.float32
+U32 = mybir.dt.uint32
+U8 = mybir.dt.uint8
+FP8X4 = mybir.dt.float8_e4m3fn_x4
+EXP = mybir.ActivationFunctionType.Exp
+MULT = mybir.AluOpType.mult
+
+P = 128
+PACK = 4
+T = 512
+HEADS = 16
+D = 128
+CHUNKS = T // P
+GROUP = 4
+GROUP_COLS = GROUP * D
+MASKED = 2.0 ** 30
+SM_BUFS = 3
+
+FLOPS = 2 * 2 * HEADS * T * T * D
+
+
+def tile_multiscaleretention_pb_kernel(tc, q_rot, k_rot, v, out):
+    nc = tc.nc
+    q_view = q_rot.rearrange("b (c p) e -> p (b c) e", p=P)
+    k_view = k_rot.rearrange("b (c p) e -> p (b c) e", p=P)
+    v_view = v.rearrange("b (c p) e -> p (b c) e", p=P)
+    out_view = out.rearrange("b (c p) e -> p (b c) e", p=P)
+
+    with ExitStack() as ctx:
+        keep = ctx.enter_context(tc.tile_pool(name="keep", bufs=1))
+        work = ctx.enter_context(tc.tile_pool(name="work", bufs=3))
+        psum_t = ctx.enter_context(tc.psum_pool(name="psum_t", bufs=2))
+        psum_s = ctx.enter_context(tc.psum_pool(name="psum_s", bufs=4))
+        psum_y = ctx.enter_context(tc.psum_pool(name="psum_y", bufs=2))
+
+        q_sb = []
+        k_sb = []
+        v_sb = []
+        for g in range(HEADS // GROUP):
+            cols = slice(g * GROUP_COLS, (g + 1) * GROUP_COLS)
+            q_g = keep.tile([P, CHUNKS, GROUP_COLS], BF16, name="q_g%d" % g)
+            k_g = keep.tile([P, CHUNKS, GROUP_COLS], BF16, name="k_g%d" % g)
+            v_g = keep.tile([P, CHUNKS, GROUP_COLS], BF16, name="v_g%d" % g)
+            nc.sync.dma_start(out=q_g[:], in_=q_view[:, :, cols])
+            nc.sync.dma_start(out=k_g[:], in_=k_view[:, :, cols])
+            nc.sync.dma_start(out=v_g[:], in_=v_view[:, :, cols])
+            q_sb.append(q_g)
+            k_sb.append(k_g)
+            v_sb.append(v_g)
+
+        ident = keep.tile([P, P], BF16, name="ident")
+        make_identity(nc, ident[:])
+
+        distance = keep.tile([P, P, CHUNKS], F32, name="distance")
+        distance_pattern = [[1, P], [-P, CHUNKS]]
+        nc.gpsimd.iota(
+            distance[:],
+            pattern=distance_pattern,
+            base=P * (CHUNKS - 1),
+            channel_multiplier=-1,
+            allow_small_or_imprecise_dtypes=True,
+        )
+        nc.gpsimd.affine_select(
+            out=distance[:],
+            in_=distance[:],
+            pattern=distance_pattern,
+            compare_op=mybir.AluOpType.is_ge,
+            fill=MASKED,
+            base=P * (CHUNKS - 1),
+            channel_multiplier=-1,
+        )
+
+        sm_tiles = []
+        for i in range(SM_BUFS):
+            sm_i = keep.tile([P, CHUNKS, P, PACK], BF16, name="sm_%d" % i, align_bytes=64)
+            nc.vector.memset(sm_i[:], 0.0)
+            sm_tiles.append(sm_i)
+
+        v_codes = keep.tile([P, HEADS * D], U32, name="v_codes", align_bytes=64)
+        v_scales = keep.tile([P, HEADS * D], U8, name="v_scales", align_bytes=64)
+
+        def quantise_v(g):
+            v_grouped = work.tile([P, GROUP_COLS, PACK], BF16, align_bytes=64)
+            nc.scalar.copy(out=v_grouped[:], in_=v_sb[g][:].rearrange("p j e -> p e j"))
+            cols = slice(g * GROUP_COLS, (g + 1) * GROUP_COLS)
+            nc.vector.quantize_mx(
+                out=v_codes[:, cols].bitcast(FP8X4),
+                scales=v_scales[:, cols],
+                in_=v_grouped[:].rearrange("p e j -> p (e j)"),
+            )
+
+        def transpose_head(h):
+            cols = slice((h % GROUP) * D, (h % GROUP + 1) * D)
+            qk_ps = psum_t.tile([P, 2 * T], BF16)
+            for c in range(CHUNKS):
+                nc.tensor.transpose(qk_ps[:, c * P : (c + 1) * P], q_sb[h // GROUP][:, c, cols], ident[:])
+            for c in range(CHUNKS):
+                nc.tensor.transpose(qk_ps[:, T + c * P : T + (c + 1) * P], k_sb[h // GROUP][:, c, cols], ident[:])
+            qk_t = work.tile([P, 2 * T], BF16)
+            nc.scalar.copy(out=qk_t[:], in_=qk_ps[:])
+            return qk_t
+
+        def decay_table(h):
+            decay = work.tile([P, P, CHUNKS], F32)
+            nc.scalar.activation(
+                out=decay[:],
+                in_=distance[:],
+                func=EXP,
+                scale=math.log(1.0 - 2.0 ** (-5 - h)),
+                bias=-0.5 * math.log(D),
+            )
+            return decay
+
+        def scores_head(h, qk_t, decay):
+            sm = sm_tiles[h % SM_BUFS]
+            for c in range(CHUNKS):
+                s_ps = psum_s.tile([P, CHUNKS, P], F32)
+                for j in range(c + 1):
+                    nc.tensor.matmul(
+                        out=s_ps[:, j, :],
+                        lhsT=qk_t[:, T + j * P : T + (j + 1) * P],
+                        rhs=qk_t[:, c * P : (c + 1) * P],
+                        start=True,
+                        stop=True,
+                    )
+                nc.vector.tensor_tensor(
+                    out=sm[:, c, :, 0 : c + 1],
+                    in0=s_ps[:, 0 : c + 1, :].rearrange("p j t -> p t j"),
+                    in1=decay[:, :, CHUNKS - 1 - c : CHUNKS],
+                    op=MULT,
+                )
+            sm_codes = work.tile([P, T], U32, align_bytes=64)
+            sm_scales = work.tile([P, T], U8, align_bytes=64)
+            nc.vector.quantize_mx(
+                out=sm_codes[:].bitcast(FP8X4),
+                scales=sm_scales[:],
+                in_=sm[:].rearrange("p c t j -> p (c t j)"),
+            )
+            return sm_codes, sm_scales
+
+        def output_head(h, sm_codes, sm_scales):
+            cols = slice(h * D, (h + 1) * D)
+            y_ps = psum_y.tile([P, CHUNKS, D], F32)
+            for c in range(CHUNKS):
+                rows = slice(c * P, (c + 1) * P)
+                nc.tensor.matmul_mx(
+                    out=y_ps[:, c, :],
+                    lhsT=sm_codes[:, rows].bitcast(FP8X4),
+                    lhsT_scale=sm_scales[:, rows],
+                    rhs=v_codes[:, cols].bitcast(FP8X4),
+                    rhs_scale=v_scales[:, cols],
+                    start=True,
+                    stop=True,
+                )
+            y_sb = work.tile([P, CHUNKS, D], F32)
+            nc.scalar.copy(out=y_sb[:], in_=y_ps[:])
+            nc.sync.dma_start(out=out_view[:, :, cols], in_=y_sb[:])
+
+        transposed = {}
+        quantised = {}
+        for step in range(HEADS + 2):
+            if step < HEADS:
+                transposed[step] = (transpose_head(step), decay_table(step))
+                if step % GROUP == 0:
+                    quantise_v(step // GROUP)
+            if 1 <= step <= HEADS:
+                qk_t, decay = transposed[step - 1]
+                quantised[step - 1] = scores_head(step - 1, qk_t, decay)
+            if step >= 2:
+                sm_codes, sm_scales = quantised[step - 2]
+                output_head(step - 2, sm_codes, sm_scales)

@@ -21,6 +21,7 @@ CHUNKS = T // P
 GROUP = 4
 GROUP_COLS = GROUP * D
 MASKED = 2.0 ** 30
+RUN = 4
 SM_BUFS = 3
 
 FLOPS = 2 * 2 * HEADS * T * T * D
@@ -88,7 +89,10 @@ def tile_multiscaleretention_pb_kernel(tc, q_rot, k_rot, v, out):
 
         def quantise_v(g):
             v_grouped = work.tile([P, GROUP_COLS, PACK], BF16, align_bytes=64)
-            nc.scalar.copy(out=v_grouped[:], in_=v_sb[g][:].rearrange("p j e -> p e j"))
+            nc.vector.tensor_copy(
+                out=v_grouped[:].rearrange("p (e i) j -> p e j i", i=RUN),
+                in_=v_sb[g][:].rearrange("p j (e i) -> p e j i", i=RUN),
+            )
             cols = slice(g * GROUP_COLS, (g + 1) * GROUP_COLS)
             nc.vector.quantize_mx(
                 out=v_codes[:, cols].bitcast(FP8X4),
@@ -120,22 +124,37 @@ def tile_multiscaleretention_pb_kernel(tc, q_rot, k_rot, v, out):
 
         def scores_head(h, qk_t, decay):
             sm = sm_tiles[h % SM_BUFS]
-            for c in range(CHUNKS):
-                s_ps = psum_s.tile([P, CHUNKS, P], F32)
-                for j in range(c + 1):
-                    nc.tensor.matmul(
-                        out=s_ps[:, j, :],
-                        lhsT=qk_t[:, T + j * P : T + (j + 1) * P],
-                        rhs=qk_t[:, c * P : (c + 1) * P],
-                        start=True,
-                        stop=True,
-                    )
-                nc.vector.tensor_tensor(
+
+            def score_block(dst, c, j):
+                nc.tensor.matmul(
+                    out=dst,
+                    lhsT=qk_t[:, T + j * P : T + (j + 1) * P],
+                    rhs=qk_t[:, c * P : (c + 1) * P],
+                    start=True,
+                    stop=True,
+                )
+
+            def mask_chunk(engine, c, s_blocks):
+                engine.tensor_tensor(
                     out=sm[:, c, :, 0 : c + 1],
-                    in0=s_ps[:, 0 : c + 1, :].rearrange("p j t -> p t j"),
+                    in0=s_blocks.rearrange("p j t -> p t j"),
                     in1=decay[:, :, CHUNKS - 1 - c : CHUNKS],
                     op=MULT,
                 )
+
+            low_ps = psum_s.tile([P, CHUNKS, P], F32, tag="s_ps")
+            score_block(low_ps[:, 0, :], 0, 0)
+            score_block(low_ps[:, 1, :], 1, 0)
+            score_block(low_ps[:, 2, :], 1, 1)
+            low_sb = work.tile([P, 3, P], F32)
+            nc.scalar.copy(out=low_sb[:], in_=low_ps[:, 0:3, :])
+            mask_chunk(nc.gpsimd, 0, low_sb[:, 0:1, :])
+            mask_chunk(nc.gpsimd, 1, low_sb[:, 1:3, :])
+            for c in range(2, CHUNKS):
+                s_ps = psum_s.tile([P, CHUNKS, P], F32, tag="s_ps")
+                for j in range(c + 1):
+                    score_block(s_ps[:, j, :], c, j)
+                mask_chunk(nc.vector, c, s_ps[:, 0 : c + 1, :])
             sm_codes = work.tile([P, T], U32, align_bytes=64)
             sm_scales = work.tile([P, T], U8, align_bytes=64)
             nc.vector.quantize_mx(

@@ -23,6 +23,7 @@ GROUP_COLS = GROUP * D
 MASKED = 2.0 ** 30
 RUN = 4
 SM_BUFS = 3
+TABLES_AHEAD = 4
 
 FLOPS = 2 * 2 * HEADS * T * T * D
 
@@ -35,6 +36,7 @@ def tile_multiscaleretention_pb_kernel(tc, q_rot, k_rot, v, out):
     out_view = out.rearrange("b (c p) e -> p (b c) e", p=P)
 
     with ExitStack() as ctx:
+        ctx.enter_context(tc.manual_schedule())
         keep = ctx.enter_context(tc.tile_pool(name="keep", bufs=1))
         work = ctx.enter_context(tc.tile_pool(name="work", bufs=3))
         psum_t = ctx.enter_context(tc.psum_pool(name="psum_t", bufs=2))
@@ -84,35 +86,18 @@ def tile_multiscaleretention_pb_kernel(tc, q_rot, k_rot, v, out):
             nc.vector.memset(sm_i[:], 0.0)
             sm_tiles.append(sm_i)
 
-        v_codes = keep.tile([P, HEADS * D], U32, name="v_codes", align_bytes=64)
-        v_scales = keep.tile([P, HEADS * D], U8, name="v_scales", align_bytes=64)
+        qk_banks = {}
+        qk_ts = {}
+        decays = {}
+        v_groupeds = {}
+        v_quantised = {}
+        sm_quantised = {}
 
-        def quantise_v(g):
-            v_grouped = work.tile([P, GROUP_COLS, PACK], BF16, align_bytes=64)
-            nc.vector.tensor_copy(
-                out=v_grouped[:].rearrange("p (e i) j -> p e j i", i=RUN),
-                in_=v_sb[g][:].rearrange("p j (e i) -> p e j i", i=RUN),
-            )
-            cols = slice(g * GROUP_COLS, (g + 1) * GROUP_COLS)
-            nc.vector.quantize_mx(
-                out=v_codes[:, cols].bitcast(FP8X4),
-                scales=v_scales[:, cols],
-                in_=v_grouped[:].rearrange("p e j -> p (e j)"),
-            )
-
-        def transpose_head(h):
-            cols = slice((h % GROUP) * D, (h % GROUP + 1) * D)
-            qk_ps = psum_t.tile([P, 2 * T], BF16)
-            for c in range(CHUNKS):
-                nc.tensor.transpose(qk_ps[:, c * P : (c + 1) * P], q_sb[h // GROUP][:, c, cols], ident[:])
-            for c in range(CHUNKS):
-                nc.tensor.transpose(qk_ps[:, T + c * P : T + (c + 1) * P], k_sb[h // GROUP][:, c, cols], ident[:])
-            qk_t = work.tile([P, 2 * T], BF16)
-            nc.scalar.copy(out=qk_t[:], in_=qk_ps[:])
-            return qk_t
+        def head_cols(h):
+            return slice((h % GROUP) * D, (h % GROUP + 1) * D)
 
         def decay_table(h):
-            decay = work.tile([P, P, CHUNKS], F32)
+            decay = keep.tile([P, P, CHUNKS], F32, name="decay_%d" % h)
             nc.scalar.activation(
                 out=decay[:],
                 in_=distance[:],
@@ -120,52 +105,88 @@ def tile_multiscaleretention_pb_kernel(tc, q_rot, k_rot, v, out):
                 scale=math.log(1.0 - 2.0 ** (-5 - h)),
                 bias=-0.5 * math.log(D),
             )
-            return decay
+            decays[h] = decay
 
-        def scores_head(h, qk_t, decay):
-            sm = sm_tiles[h % SM_BUFS]
-
-            def score_block(dst, c, j):
-                nc.tensor.matmul(
-                    out=dst,
-                    lhsT=qk_t[:, T + j * P : T + (j + 1) * P],
-                    rhs=qk_t[:, c * P : (c + 1) * P],
-                    start=True,
-                    stop=True,
+        def transpose_head(h):
+            qk_ps = psum_t.tile([P, 2 * T], BF16)
+            for c in range(CHUNKS):
+                nc.tensor.transpose(qk_ps[:, c * P : (c + 1) * P], q_sb[h // GROUP][:, c, head_cols(h)], ident[:])
+            for c in range(CHUNKS):
+                nc.tensor.transpose(
+                    qk_ps[:, T + c * P : T + (c + 1) * P], k_sb[h // GROUP][:, c, head_cols(h)], ident[:]
                 )
+            qk_banks[h] = qk_ps
 
-            def mask_chunk(engine, c, s_blocks):
-                engine.tensor_tensor(
-                    out=sm[:, c, :, 0 : c + 1],
-                    in0=s_blocks.rearrange("p j t -> p t j"),
-                    in1=decay[:, :, CHUNKS - 1 - c : CHUNKS],
-                    op=MULT,
-                )
+        def copy_transposed(h):
+            qk_t = work.tile([P, 2 * T], BF16)
+            nc.scalar.copy(out=qk_t[:], in_=qk_banks[h][:])
+            qk_ts[h] = qk_t
 
+        def score_block(h, dst, c, j):
+            qk_t = qk_ts[h]
+            nc.tensor.matmul(
+                out=dst,
+                lhsT=qk_t[:, T + j * P : T + (j + 1) * P],
+                rhs=qk_t[:, c * P : (c + 1) * P],
+                start=True,
+                stop=True,
+            )
+
+        def mask_chunk(engine, h, c, s_blocks):
+            engine.tensor_tensor(
+                out=sm_tiles[h % SM_BUFS][:, c, :, 0 : c + 1],
+                in0=s_blocks.rearrange("p j t -> p t j"),
+                in1=decays[h][:, :, CHUNKS - 1 - c : CHUNKS],
+                op=MULT,
+            )
+
+        def low_chunks(h):
             low_ps = psum_s.tile([P, CHUNKS, P], F32, tag="s_ps")
-            score_block(low_ps[:, 0, :], 0, 0)
-            score_block(low_ps[:, 1, :], 1, 0)
-            score_block(low_ps[:, 2, :], 1, 1)
+            score_block(h, low_ps[:, 0, :], 0, 0)
+            score_block(h, low_ps[:, 1, :], 1, 0)
+            score_block(h, low_ps[:, 2, :], 1, 1)
             low_sb = work.tile([P, 3, P], F32)
             nc.scalar.copy(out=low_sb[:], in_=low_ps[:, 0:3, :])
-            mask_chunk(nc.gpsimd, 0, low_sb[:, 0:1, :])
-            mask_chunk(nc.gpsimd, 1, low_sb[:, 1:3, :])
-            for c in range(2, CHUNKS):
-                s_ps = psum_s.tile([P, CHUNKS, P], F32, tag="s_ps")
-                for j in range(c + 1):
-                    score_block(s_ps[:, j, :], c, j)
-                mask_chunk(nc.vector, c, s_ps[:, 0 : c + 1, :])
+            mask_chunk(nc.gpsimd, h, 0, low_sb[:, 0:1, :])
+            mask_chunk(nc.gpsimd, h, 1, low_sb[:, 1:3, :])
+
+        def high_chunk(h, c):
+            s_ps = psum_s.tile([P, CHUNKS, P], F32, tag="s_ps")
+            for j in range(c + 1):
+                score_block(h, s_ps[:, j, :], c, j)
+            mask_chunk(nc.vector, h, c, s_ps[:, 0 : c + 1, :])
+
+        def quantise_sm(h):
             sm_codes = work.tile([P, T], U32, align_bytes=64)
             sm_scales = work.tile([P, T], U8, align_bytes=64)
             nc.vector.quantize_mx(
                 out=sm_codes[:].bitcast(FP8X4),
                 scales=sm_scales[:],
-                in_=sm[:].rearrange("p c t j -> p (c t j)"),
+                in_=sm_tiles[h % SM_BUFS][:].rearrange("p c t j -> p (c t j)"),
             )
-            return sm_codes, sm_scales
+            sm_quantised[h] = (sm_codes, sm_scales)
 
-        def output_head(h, sm_codes, sm_scales):
-            cols = slice(h * D, (h + 1) * D)
+        def regroup_v(h):
+            v_grouped = work.tile([P, D, PACK], BF16, align_bytes=64)
+            nc.vector.tensor_copy(
+                out=v_grouped[:].rearrange("p (e i) j -> p e j i", i=RUN),
+                in_=v_sb[h // GROUP][:, :, head_cols(h)].rearrange("p j (e i) -> p e j i", i=RUN),
+            )
+            v_groupeds[h] = v_grouped
+
+        def quantise_v(h):
+            v_codes = work.tile([P, D], U32, align_bytes=64, bufs=4)
+            v_scales = work.tile([P, D], U8, align_bytes=64, bufs=4)
+            nc.vector.quantize_mx(
+                out=v_codes[:].bitcast(FP8X4),
+                scales=v_scales[:],
+                in_=v_groupeds[h][:].rearrange("p e j -> p (e j)"),
+            )
+            v_quantised[h] = (v_codes, v_scales)
+
+        def output_head(h):
+            sm_codes, sm_scales = sm_quantised[h]
+            v_codes, v_scales = v_quantised[h]
             y_ps = psum_y.tile([P, CHUNKS, D], F32)
             for c in range(CHUNKS):
                 rows = slice(c * P, (c + 1) * P)
@@ -173,25 +194,36 @@ def tile_multiscaleretention_pb_kernel(tc, q_rot, k_rot, v, out):
                     out=y_ps[:, c, :],
                     lhsT=sm_codes[:, rows].bitcast(FP8X4),
                     lhsT_scale=sm_scales[:, rows],
-                    rhs=v_codes[:, cols].bitcast(FP8X4),
-                    rhs_scale=v_scales[:, cols],
+                    rhs=v_codes[:].bitcast(FP8X4),
+                    rhs_scale=v_scales[:],
                     start=True,
                     stop=True,
                 )
             y_sb = work.tile([P, CHUNKS, D], F32)
             nc.scalar.copy(out=y_sb[:], in_=y_ps[:])
-            nc.sync.dma_start(out=out_view[:, :, cols], in_=y_sb[:])
+            nc.sync.dma_start(out=out_view[:, :, h * D : (h + 1) * D], in_=y_sb[:])
 
-        transposed = {}
-        quantised = {}
-        for step in range(HEADS + 2):
-            if step < HEADS:
-                transposed[step] = (transpose_head(step), decay_table(step))
-                if step % GROUP == 0:
-                    quantise_v(step // GROUP)
-            if 1 <= step <= HEADS:
-                qk_t, decay = transposed[step - 1]
-                quantised[step - 1] = scores_head(step - 1, qk_t, decay)
-            if step >= 2:
-                sm_codes, sm_scales = quantised[step - 2]
-                output_head(step - 2, sm_codes, sm_scales)
+        def is_head(h):
+            return 0 <= h < HEADS
+
+        for h in range(TABLES_AHEAD):
+            decay_table(h)
+        for s in range(-1, HEADS + 3):
+            if is_head(s):
+                copy_transposed(s)
+            if is_head(s - 1):
+                low_chunks(s - 1)
+                high_chunk(s - 1, 2)
+            if is_head(s - 2):
+                quantise_sm(s - 2)
+            if is_head(s - 1):
+                high_chunk(s - 1, 3)
+                quantise_v(s - 1)
+            if is_head(s):
+                regroup_v(s)
+            if is_head(s + TABLES_AHEAD) and s >= 0:
+                decay_table(s + TABLES_AHEAD)
+            if is_head(s + 1):
+                transpose_head(s + 1)
+            if is_head(s - 3):
+                output_head(s - 3)

@@ -18,7 +18,7 @@ T = 512
 HEADS = 16
 D = 128
 CHUNKS = T // P
-GROUP = 4
+GROUP = 2
 GROUP_COLS = GROUP * D
 MASKED = 2.0 ** 30
 RUN = 4
@@ -168,7 +168,7 @@ def tile_multiscaleretention_pb_kernel(tc, q_rot, k_rot, v, out):
 
         def regroup_v(h):
             v_grouped = work.tile([P, D, PACK], BF16, align_bytes=64)
-            nc.vector.tensor_copy(
+            nc.scalar.copy(
                 out=v_grouped[:].rearrange("p (e i) j -> p e j i", i=RUN),
                 in_=v_sb[h // GROUP][:, :, head_cols(h)].rearrange("p j (e i) -> p e j i", i=RUN),
             )
@@ -200,7 +200,10 @@ def tile_multiscaleretention_pb_kernel(tc, q_rot, k_rot, v, out):
                     stop=True,
                 )
             y_sb = work.tile([P, CHUNKS, D], F32)
-            nc.scalar.copy(out=y_sb[:], in_=y_ps[:])
+            if h % 2 == 0:
+                nc.scalar.copy(out=y_sb[:], in_=y_ps[:])
+            else:
+                nc.vector.tensor_copy(out=y_sb[:], in_=y_ps[:])
             nc.sync.dma_start(out=out_view[:, :, h * D : (h + 1) * D], in_=y_sb[:])
 
         def is_head(h):

@@ -20,6 +20,8 @@ D = 128
 CHUNKS = T // P
 GROUP = 2
 GROUP_COLS = GROUP * D
+V_GROUP = 4
+V_GROUP_COLS = V_GROUP * D
 MASKED = 2.0 ** 30
 RUN = 4
 SM_BUFS = 3
@@ -50,16 +52,15 @@ def tile_multiscaleretention_pb_kernel(tc, q_rot, k_rot, v, out):
             cols = slice(g * GROUP_COLS, (g + 1) * GROUP_COLS)
             q_g = keep.tile([P, CHUNKS, GROUP_COLS], BF16, name="q_g%d" % g)
             k_g = keep.tile([P, CHUNKS, GROUP_COLS], BF16, name="k_g%d" % g)
-            v_g = keep.tile([P, CHUNKS, GROUP_COLS], BF16, name="v_g%d" % g)
             nc.sync.dma_start(out=q_g[:], in_=q_view[:, :, cols])
             nc.sync.dma_start(out=k_g[:], in_=k_view[:, :, cols])
-            nc.sync.dma_start(out=v_g[:], in_=v_view[:, :, cols])
             q_sb.append(q_g)
             k_sb.append(k_g)
-            v_sb.append(v_g)
-
-        ident = keep.tile([P, P], BF16, name="ident")
-        make_identity(nc, ident[:])
+            if (g * GROUP) % V_GROUP == 0:
+                first = g * GROUP_COLS
+                v_g = keep.tile([P, CHUNKS, V_GROUP_COLS], BF16, name="v_g%d" % len(v_sb))
+                nc.sync.dma_start(out=v_g[:], in_=v_view[:, :, first : first + V_GROUP_COLS])
+                v_sb.append(v_g)
 
         distance = keep.tile([P, P, CHUNKS], F32, name="distance")
         distance_pattern = [[1, P], [-P, CHUNKS]]
@@ -80,17 +81,22 @@ def tile_multiscaleretention_pb_kernel(tc, q_rot, k_rot, v, out):
             channel_multiplier=-1,
         )
 
+        ident = keep.tile([P, P], BF16, name="ident")
+        make_identity(nc, ident[:])
+
         sm_tiles = []
         for i in range(SM_BUFS):
             sm_i = keep.tile([P, CHUNKS, P, PACK], BF16, name="sm_%d" % i, align_bytes=64)
             nc.vector.memset(sm_i[:], 0.0)
             sm_tiles.append(sm_i)
 
+        v_codes = keep.tile([P, HEADS * D], U32, name="v_codes", align_bytes=64)
+        v_scales = keep.tile([P, HEADS * D], U8, name="v_scales", align_bytes=64)
+
         qk_banks = {}
         qk_ts = {}
         decays = {}
         v_groupeds = {}
-        v_quantised = {}
         sm_quantised = {}
 
         def head_cols(h):
@@ -166,27 +172,25 @@ def tile_multiscaleretention_pb_kernel(tc, q_rot, k_rot, v, out):
             )
             sm_quantised[h] = (sm_codes, sm_scales)
 
-        def regroup_v(h):
-            v_grouped = work.tile([P, D, PACK], BF16, align_bytes=64)
-            nc.scalar.copy(
+        def regroup_v(g):
+            v_grouped = work.tile([P, V_GROUP_COLS, PACK], BF16, align_bytes=64, bufs=2)
+            nc.vector.tensor_copy(
                 out=v_grouped[:].rearrange("p (e i) j -> p e j i", i=RUN),
-                in_=v_sb[h // GROUP][:, :, head_cols(h)].rearrange("p j (e i) -> p e j i", i=RUN),
+                in_=v_sb[g][:].rearrange("p j (e i) -> p e j i", i=RUN),
             )
-            v_groupeds[h] = v_grouped
+            v_groupeds[g] = v_grouped
 
-        def quantise_v(h):
-            v_codes = work.tile([P, D], U32, align_bytes=64, bufs=4)
-            v_scales = work.tile([P, D], U8, align_bytes=64, bufs=4)
+        def quantise_v(g):
+            cols = slice(g * V_GROUP_COLS, (g + 1) * V_GROUP_COLS)
             nc.vector.quantize_mx(
-                out=v_codes[:].bitcast(FP8X4),
-                scales=v_scales[:],
-                in_=v_groupeds[h][:].rearrange("p e j -> p (e j)"),
+                out=v_codes[:, cols].bitcast(FP8X4),
+                scales=v_scales[:, cols],
+                in_=v_groupeds[g][:].rearrange("p e j -> p (e j)"),
             )
-            v_quantised[h] = (v_codes, v_scales)
 
         def output_head(h):
             sm_codes, sm_scales = sm_quantised[h]
-            v_codes, v_scales = v_quantised[h]
+            cols = slice(h * D, (h + 1) * D)
             y_ps = psum_y.tile([P, CHUNKS, D], F32)
             for c in range(CHUNKS):
                 rows = slice(c * P, (c + 1) * P)
@@ -194,17 +198,14 @@ def tile_multiscaleretention_pb_kernel(tc, q_rot, k_rot, v, out):
                     out=y_ps[:, c, :],
                     lhsT=sm_codes[:, rows].bitcast(FP8X4),
                     lhsT_scale=sm_scales[:, rows],
-                    rhs=v_codes[:].bitcast(FP8X4),
-                    rhs_scale=v_scales[:],
+                    rhs=v_codes[:, cols].bitcast(FP8X4),
+                    rhs_scale=v_scales[:, cols],
                     start=True,
                     stop=True,
                 )
             y_sb = work.tile([P, CHUNKS, D], F32)
-            if h % 2 == 0:
-                nc.scalar.copy(out=y_sb[:], in_=y_ps[:])
-            else:
-                nc.vector.tensor_copy(out=y_sb[:], in_=y_ps[:])
-            nc.sync.dma_start(out=out_view[:, :, h * D : (h + 1) * D], in_=y_sb[:])
+            nc.scalar.copy(out=y_sb[:], in_=y_ps[:])
+            nc.sync.dma_start(out=out_view[:, :, cols], in_=y_sb[:])
 
         def is_head(h):
             return 0 <= h < HEADS
@@ -217,16 +218,17 @@ def tile_multiscaleretention_pb_kernel(tc, q_rot, k_rot, v, out):
             if is_head(s - 1):
                 low_chunks(s - 1)
                 high_chunk(s - 1, 2)
+            if is_head(s - 3):
+                output_head(s - 3)
             if is_head(s - 2):
                 quantise_sm(s - 2)
             if is_head(s - 1):
                 high_chunk(s - 1, 3)
-                quantise_v(s - 1)
-            if is_head(s):
-                regroup_v(s)
+            if is_head(s) and s % V_GROUP == 0:
+                quantise_v(s // V_GROUP)
+            if is_head(s + 1) and (s + 1) % V_GROUP == 0:
+                regroup_v((s + 1) // V_GROUP)
             if is_head(s + TABLES_AHEAD) and s >= 0:
                 decay_table(s + TABLES_AHEAD)
             if is_head(s + 1):
                 transpose_head(s + 1)
-            if is_head(s - 3):
-                output_head(s - 3)

import math
from contextlib import ExitStack

import concourse.mybir as mybir
from concourse.masks import make_identity

BF16 = mybir.dt.bfloat16
F32 = mybir.dt.float32
U32 = mybir.dt.uint32
U8 = mybir.dt.uint8
FP8X4 = mybir.dt.float8_e4m3fn_x4
EXP = mybir.ActivationFunctionType.Exp
MULT = mybir.AluOpType.mult

P = 128
PACK = 4
T = 512
HEADS = 16
D = 128
CHUNKS = T // P
GROUP = 2
GROUP_COLS = GROUP * D
V_GROUP = 4
V_GROUP_COLS = V_GROUP * D
MASKED = 2.0 ** 30
RUN = 4
SM_BUFS = 3
TABLES_AHEAD = 4

FLOPS = 2 * 2 * HEADS * T * T * D


def tile_multiscaleretention_pb_kernel(tc, q_rot, k_rot, v, out):
    nc = tc.nc
    q_view = q_rot.rearrange("b (c p) e -> p (b c) e", p=P)
    k_view = k_rot.rearrange("b (c p) e -> p (b c) e", p=P)
    v_view = v.rearrange("b (c p) e -> p (b c) e", p=P)
    out_view = out.rearrange("b (c p) e -> p (b c) e", p=P)

    with ExitStack() as ctx:
        ctx.enter_context(tc.manual_schedule())
        keep = ctx.enter_context(tc.tile_pool(name="keep", bufs=1))
        work = ctx.enter_context(tc.tile_pool(name="work", bufs=3))
        psum_t = ctx.enter_context(tc.psum_pool(name="psum_t", bufs=2))
        psum_s = ctx.enter_context(tc.psum_pool(name="psum_s", bufs=4))
        psum_y = ctx.enter_context(tc.psum_pool(name="psum_y", bufs=2))

        q_sb = []
        k_sb = []
        v_sb = []
        for g in range(HEADS // GROUP):
            cols = slice(g * GROUP_COLS, (g + 1) * GROUP_COLS)
            q_g = keep.tile([P, CHUNKS, GROUP_COLS], BF16, name="q_g%d" % g)
            k_g = keep.tile([P, CHUNKS, GROUP_COLS], BF16, name="k_g%d" % g)
            nc.sync.dma_start(out=q_g[:], in_=q_view[:, :, cols])
            nc.sync.dma_start(out=k_g[:], in_=k_view[:, :, cols])
            q_sb.append(q_g)
            k_sb.append(k_g)
            if (g * GROUP) % V_GROUP == 0:
                first = g * GROUP_COLS
                v_g = keep.tile([P, CHUNKS, V_GROUP_COLS], BF16, name="v_g%d" % len(v_sb))
                nc.sync.dma_start(out=v_g[:], in_=v_view[:, :, first : first + V_GROUP_COLS])
                v_sb.append(v_g)

        distance = keep.tile([P, P, CHUNKS], F32, name="distance")
        distance_pattern = [[1, P], [-P, CHUNKS]]
        nc.gpsimd.iota(
            distance[:],
            pattern=distance_pattern,
            base=P * (CHUNKS - 1),
            channel_multiplier=-1,
            allow_small_or_imprecise_dtypes=True,
        )
        nc.gpsimd.affine_select(
            out=distance[:],
            in_=distance[:],
            pattern=distance_pattern,
            compare_op=mybir.AluOpType.is_ge,
            fill=MASKED,
            base=P * (CHUNKS - 1),
            channel_multiplier=-1,
        )

        ident = keep.tile([P, P], BF16, name="ident")
        make_identity(nc, ident[:])

        sm_tiles = []
        for i in range(SM_BUFS):
            sm_i = keep.tile([P, CHUNKS, P, PACK], BF16, name="sm_%d" % i, align_bytes=64)
            nc.vector.memset(sm_i[:], 0.0)
            sm_tiles.append(sm_i)

        v_codes = keep.tile([P, HEADS * D], U32, name="v_codes", align_bytes=64)
        v_scales = keep.tile([P, HEADS * D], U8, name="v_scales", align_bytes=64)

        qk_banks = {}
        qk_ts = {}
        decays = {}
        v_groupeds = {}
        sm_quantised = {}

        def head_cols(h):
            return slice((h % GROUP) * D, (h % GROUP + 1) * D)

        def decay_table(h):
            decay = keep.tile([P, P, CHUNKS], F32, name="decay_%d" % h)
            nc.scalar.activation(
                out=decay[:],
                in_=distance[:],
                func=EXP,
                scale=math.log(1.0 - 2.0 ** (-5 - h)),
                bias=-0.5 * math.log(D),
            )
            decays[h] = decay

        def transpose_head(h):
            qk_ps = psum_t.tile([P, 2 * T], BF16)
            for c in range(CHUNKS):
                nc.tensor.transpose(qk_ps[:, c * P : (c + 1) * P], q_sb[h // GROUP][:, c, head_cols(h)], ident[:])
            for c in range(CHUNKS):
                nc.tensor.transpose(
                    qk_ps[:, T + c * P : T + (c + 1) * P], k_sb[h // GROUP][:, c, head_cols(h)], ident[:]
                )
            qk_banks[h] = qk_ps

        def copy_transposed(h):
            qk_t = work.tile([P, 2 * T], BF16)
            nc.scalar.copy(out=qk_t[:], in_=qk_banks[h][:])
            qk_ts[h] = qk_t

        def score_block(h, dst, c, j):
            qk_t = qk_ts[h]
            nc.tensor.matmul(
                out=dst,
                lhsT=qk_t[:, T + j * P : T + (j + 1) * P],
                rhs=qk_t[:, c * P : (c + 1) * P],
                start=True,
                stop=True,
            )

        def mask_chunk(engine, h, c, s_blocks):
            engine.tensor_tensor(
                out=sm_tiles[h % SM_BUFS][:, c, :, 0 : c + 1],
                in0=s_blocks.rearrange("p j t -> p t j"),
                in1=decays[h][:, :, CHUNKS - 1 - c : CHUNKS],
                op=MULT,
            )

        def low_chunks(h):
            low_ps = psum_s.tile([P, CHUNKS, P], F32, tag="s_ps")
            score_block(h, low_ps[:, 0, :], 0, 0)
            score_block(h, low_ps[:, 1, :], 1, 0)
            score_block(h, low_ps[:, 2, :], 1, 1)
            low_sb = work.tile([P, 3, P], F32)
            nc.scalar.copy(out=low_sb[:], in_=low_ps[:, 0:3, :])
            mask_chunk(nc.gpsimd, h, 0, low_sb[:, 0:1, :])
            mask_chunk(nc.gpsimd, h, 1, low_sb[:, 1:3, :])

        def high_chunk(h, c):
            s_ps = psum_s.tile([P, CHUNKS, P], F32, tag="s_ps")
            for j in range(c + 1):
                score_block(h, s_ps[:, j, :], c, j)
            mask_chunk(nc.vector, h, c, s_ps[:, 0 : c + 1, :])

        def quantise_sm(h):
            sm_codes = work.tile([P, T], U32, align_bytes=64)
            sm_scales = work.tile([P, T], U8, align_bytes=64)
            nc.vector.quantize_mx(
                out=sm_codes[:].bitcast(FP8X4),
                scales=sm_scales[:],
                in_=sm_tiles[h % SM_BUFS][:].rearrange("p c t j -> p (c t j)"),
            )
            sm_quantised[h] = (sm_codes, sm_scales)

        def regroup_v(g):
            v_grouped = work.tile([P, V_GROUP_COLS, PACK], BF16, align_bytes=64, bufs=2)
            nc.vector.tensor_copy(
                out=v_grouped[:].rearrange("p (e i) j -> p e j i", i=RUN),
                in_=v_sb[g][:].rearrange("p j (e i) -> p e j i", i=RUN),
            )
            v_groupeds[g] = v_grouped

        def quantise_v(g):
            cols = slice(g * V_GROUP_COLS, (g + 1) * V_GROUP_COLS)
            nc.vector.quantize_mx(
                out=v_codes[:, cols].bitcast(FP8X4),
                scales=v_scales[:, cols],
                in_=v_groupeds[g][:].rearrange("p e j -> p (e j)"),
            )

        def output_head(h):
            sm_codes, sm_scales = sm_quantised[h]
            cols = slice(h * D, (h + 1) * D)
            y_ps = psum_y.tile([P, CHUNKS, D], F32)
            for c in range(CHUNKS):
                rows = slice(c * P, (c + 1) * P)
                nc.tensor.matmul_mx(
                    out=y_ps[:, c, :],
                    lhsT=sm_codes[:, rows].bitcast(FP8X4),
                    lhsT_scale=sm_scales[:, rows],
                    rhs=v_codes[:, cols].bitcast(FP8X4),
                    rhs_scale=v_scales[:, cols],
                    start=True,
                    stop=True,
                )
            y_sb = work.tile([P, CHUNKS, D], F32)
            nc.scalar.copy(out=y_sb[:], in_=y_ps[:])
            nc.sync.dma_start(out=out_view[:, :, cols], in_=y_sb[:])

        def is_head(h):
            return 0 <= h < HEADS

        for h in range(TABLES_AHEAD):
            decay_table(h)
        for s in range(-1, HEADS + 3):
            if is_head(s):
                copy_transposed(s)
            if is_head(s - 1):
                low_chunks(s - 1)
                high_chunk(s - 1, 2)
            if is_head(s - 3):
                output_head(s - 3)
            if is_head(s - 2):
                quantise_sm(s - 2)
            if is_head(s - 1):
                high_chunk(s - 1, 3)
            if is_head(s) and s % V_GROUP == 0:
                quantise_v(s // V_GROUP)
            if is_head(s + 1) and (s + 1) % V_GROUP == 0:
                regroup_v((s + 1) // V_GROUP)
            if is_head(s + TABLES_AHEAD) and s >= 0:
                decay_table(s + TABLES_AHEAD)
            if is_head(s + 1):
                transpose_head(s + 1)
